import numpy as np
import ml_dtypes


def mxq(x, axis, fmt="e4m3"):
    dtype, down = {"e4m3": (ml_dtypes.float8_e4m3fn, 7), "e5m2": (ml_dtypes.float8_e5m2, 14)}[fmt]
    v = np.moveaxis(np.asarray(x, np.float32).astype(ml_dtypes.bfloat16).astype(np.float64), axis, -1)
    blocks = v.reshape(v.shape[:-1] + (-1, 32))
    amax = np.abs(blocks).max(-1, keepdims=True)
    byte = np.maximum(np.where(amax > 0, np.frexp(amax)[1] - 1 + 127, 0) - down, 1)
    scale = np.exp2(byte - 127.0)
    codes = (blocks / scale).astype(np.float32).astype(dtype).astype(np.float64)
    return np.moveaxis((codes * scale).reshape(v.shape), -1, axis)


WIDE = False


def mx_kscale(k):
    if not WIDE:
        return np.ones(k)
    levels = np.array([10, -10, 5, -5, 0])
    a = np.random.permutation(np.resize(levels, k // 512 * 4)).reshape(k // 512, 4)
    idx = np.arange(k)
    return np.exp2(a[idx // 512, idx % 128 // 32])


BF16 = ml_dtypes.bfloat16


def bf(x):
    return np.asarray(x, np.float32).astype(BF16)


def f64(x):
    return np.asarray(x).astype(np.float64)


B, C, N, T, Q = 4, 128, 512, 8, 4


def setup_inputs():
    s = mx_kscale(N)
    a = 2.0 / np.sqrt(N)
    return {"x": bf(np.random.standard_normal((B, C, N, T)) * s[:, None]),
            "Ar": bf(np.random.uniform(0.0, 1.0, (N, N)) * a / s),
            "Ai": bf(np.random.uniform(0.0, 1.0, (N, N)) * a / s),
            "Aj": bf(np.random.uniform(0.0, 1.0, (N, N)) * a / s),
            "Ak": bf(np.random.uniform(0.0, 1.0, (N, N)) * a / s)}


def reference(x, Ar, Ai, Aj, Ak):
    xq = mxq(f64(x), 2, "e4m3")
    Yr = mxq(f64(Ar), 1, "e4m3") @ xq
    Yi = mxq(f64(Ai), 1, "e4m3") @ xq
    Yj = mxq(f64(Aj), 1, "e4m3") @ xq
    Yk = mxq(f64(Ak), 1, "e4m3") @ xq
    Yr_r, Yr_i, Yr_j, Yr_k = np.split(Yr, Q, axis=1)
    Yi_r, Yi_i, Yi_j, Yi_k = np.split(Yi, Q, axis=1)
    Yj_r, Yj_i, Yj_j, Yj_k = np.split(Yj, Q, axis=1)
    Yk_r, Yk_i, Yk_j, Yk_k = np.split(Yk, Q, axis=1)
    out_r = Yr_r - Yi_i - Yj_j - Yk_k
    out_i = Yr_i + Yi_r + Yj_k - Yk_j
    out_j = Yr_j - Yi_k + Yj_r + Yk_i
    out_k = Yr_k + Yi_j - Yj_i + Yk_r
    return np.concatenate([out_r, out_i, out_j, out_k], axis=1)

@@ -1,0 +1,201 @@
+from contextlib import ExitStack
+
+import concourse.mybir as mybir
+from concourse.masks import make_identity
+
+F32 = mybir.dt.float32
+BF16 = mybir.dt.bfloat16
+U32 = mybir.dt.uint32
+U8 = mybir.dt.uint8
+FP8X4 = mybir.dt.float8_e4m3fn_x4
+
+B, C, N, T, Q = 4, 128, 512, 8, 4
+P = 128
+PACK = 4
+GROUP = C // Q
+N_TILES = N // P
+T_BANK = 4
+T_HALVES = T // T_BANK
+BANK = 512
+
+SIGN = (
+    (+1, -1, -1, -1),
+    (+1, +1, +1, -1),
+    (+1, -1, +1, +1),
+    (+1, +1, -1, +1),
+)
+SLOTS = 2 * Q - 1
+SLOT_RUNS = ((0, 4), (4, 2), (6, 1))
+
+FLOPS = 2 * Q * N * N * B * C * T
+
+
+def slot_of(g, a):
+    return a if SIGN[g][a] > 0 else Q - 1 + a
+
+
+def tile_nconv_pa_t_kernel(tc, x, Ar, Ai, Aj, Ak, out):
+    nc = tc.nc
+    adjacency = (Ar, Ai, Aj, Ak)
+
+    with ExitStack() as stack:
+        keep = stack.enter_context(tc.tile_pool(name="keep", bufs=1))
+        a_stage = stack.enter_context(tc.tile_pool(name="a_stage", bufs=2))
+        o_stage = stack.enter_context(tc.tile_pool(name="o_stage", bufs=4))
+        psum = stack.enter_context(tc.psum_pool(name="psum", bufs=4))
+
+        ident = keep.tile([P, P], F32)
+        make_identity(nc, ident[:])
+
+        def load_adjacency(nt):
+            tiles = []
+            for a in range(Q):
+                raw = keep.tile([P, N], BF16, name="a_raw_%d_%d" % (nt, a))
+                nc.sync.dma_start(out=raw[:], in_=adjacency[a][nt * P : (nt + 1) * P, :])
+                tiles.append(raw)
+            return tiles
+
+        a_raw = [load_adjacency(0)]
+        x_raw = []
+        for g in range(Q):
+            raw = keep.tile([P, N * T], BF16, name="x_raw_%d" % g)
+            for b in range(B):
+                nc.sync.dma_start(
+                    out=raw[b:P:B, :],
+                    in_=x[b, g * GROUP : (g + 1) * GROUP].rearrange("c m t -> c (m t)"),
+                )
+            x_raw.append(raw)
+        for nt in range(1, N_TILES):
+            a_raw.append(load_adjacency(nt))
+
+        x_grouped = [
+            keep.tile([P, T * P * PACK], BF16, name="x_grouped_%d" % g, align_bytes=64)
+            for g in range(Q)
+        ]
+        x_codes = [
+            [
+                keep.tile([P, T_BANK * P], U32, name="x_codes_%d_%d" % (g, h), align_bytes=64)
+                for h in range(T_HALVES)
+            ]
+            for g in range(Q)
+        ]
+        x_scales = [
+            [
+                keep.tile([P, T_BANK * P], U8, name="x_scales_%d_%d" % (g, h), align_bytes=64)
+                for h in range(T_HALVES)
+            ]
+            for g in range(Q)
+        ]
+
+        def regroup_x(g, h):
+            words = x_raw[g][:].bitcast(F32).rearrange(
+                "p (u q e w) -> p u q e w", u=2, q=P, e=2, w=T // 2
+            )
+            grouped = x_grouped[g][:].rearrange("p (t c j) -> p t c j", t=T, c=P, j=PACK)
+            for w in range(2 * h, 2 * h + 2):
+                bank = psum.tile([P, BANK], F32, tag="transposed")
+                for u in range(2):
+                    for e in range(2):
+                        j = 2 * u + e
+                        nc.tensor.transpose(
+                            bank[:, j * P : (j + 1) * P], words[:, u, :, e, w], ident[:]
+                        )
+                halves = bank[:].bitcast(BF16).rearrange(
+                    "p (j c s) -> p s c j", j=PACK, c=P, s=2
+                )
+                if w % 2 == 0:
+                    nc.scalar.copy(out=grouped[:, 2 * w : 2 * w + 2, :, :], in_=halves)
+                else:
+                    nc.vector.tensor_copy(out=grouped[:, 2 * w : 2 * w + 2, :, :], in_=halves)
+
+        def quantise_x(g, h):
+            width = T_BANK * P * PACK
+            nc.vector.quantize_mx(
+                out=x_codes[g][h][:].bitcast(FP8X4),
+                scales=x_scales[g][h][:],
+                in_=x_grouped[g][:, h * width : (h + 1) * width],
+            )
+
+        a_codes = [
+            keep.tile([P, SLOTS * P], U32, name="a_codes_%d" % nt, align_bytes=64)
+            for nt in range(N_TILES)
+        ]
+        a_scales = [
+            keep.tile([P, SLOTS * P], U8, name="a_scales_%d" % nt, align_bytes=64)
+            for nt in range(N_TILES)
+        ]
+
+        def prepare_adjacency(nt):
+            grouped = a_stage.tile([P, SLOTS * P * PACK], BF16, align_bytes=64)
+            grouped_words = grouped[:].bitcast(F32).rearrange(
+                "p (s n u) -> p s n u", s=SLOTS, n=P, u=2
+            )
+            for pair in range(2):
+                bank = psum.tile([P, BANK], F32, tag="transposed")
+                for i in range(2):
+                    words = a_raw[nt][2 * pair + i][:].bitcast(F32)
+                    for u in range(2):
+                        k = 2 * i + u
+                        nc.tensor.transpose(
+                            bank[:, k * P : (k + 1) * P], words[:, u * P : (u + 1) * P], ident[:]
+                        )
+                nc.scalar.copy(
+                    out=grouped_words[:, 2 * pair : 2 * pair + 2, :, :],
+                    in_=bank[:].rearrange("p (s u n) -> p s n u", s=2, u=2, n=P),
+                )
+            slot_width = P * PACK
+            nc.vector.tensor_scalar_mul(
+                out=grouped[:, Q * slot_width : SLOTS * slot_width],
+                in0=grouped[:, slot_width : Q * slot_width],
+                scalar1=-1.0,
+            )
+            for first, count in SLOT_RUNS:
+                nc.vector.quantize_mx(
+                    out=a_codes[nt][:, first * P : (first + count) * P].bitcast(FP8X4),
+                    scales=a_scales[nt][:, first * P : (first + count) * P],
+                    in_=grouped[:, first * slot_width : (first + count) * slot_width],
+                )
+
+        def multiply(nt, g):
+            result = o_stage.tile([P, P * T], F32)
+            result_nt = result[:].rearrange("p (n t) -> p n t", n=P, t=T)
+            for h in range(T_HALVES):
+                acc = psum.tile([P, BANK], F32, tag="acc")
+                for tl in range(T_BANK):
+                    for a in range(Q):
+                        s = slot_of(g, a)
+                        nc.tensor.matmul_mx(
+                            out=acc[:, tl * P : (tl + 1) * P],
+                            lhsT=x_codes[g ^ a][h][:, tl * P : (tl + 1) * P].bitcast(FP8X4),
+                            lhsT_scale=x_scales[g ^ a][h][:, tl * P : (tl + 1) * P],
+                            rhs=a_codes[nt][:, s * P : (s + 1) * P].bitcast(FP8X4),
+                            rhs_scale=a_scales[nt][:, s * P : (s + 1) * P],
+                            start=(a == 0),
+                            stop=(a == Q - 1),
+                        )
+                by_node = acc[:].rearrange("p (t n) -> p n t", t=T_BANK, n=P)
+                target = result_nt[:, :, h * T_BANK : (h + 1) * T_BANK]
+                if (nt * Q + g) % 2 == 0:
+                    nc.scalar.copy(out=target, in_=by_node)
+                else:
+                    nc.vector.tensor_copy(out=target, in_=by_node)
+            for b in range(B):
+                nc.sync.dma_start(
+                    out=out[
+                        b, g * GROUP : (g + 1) * GROUP, nt * P : (nt + 1) * P, :
+                    ].rearrange("c n t -> c (n t)"),
+                    in_=result[b:P:B, :],
+                )
+
+        prepare_adjacency(0)
+        units = [(g, h) for g in range(Q) for h in range(T_HALVES)]
+        for k, (g, h) in enumerate(units):
+            regroup_x(g, h)
+            if k > 0:
+                quantise_x(*units[k - 1])
+        quantise_x(*units[-1])
+        for nt in range(N_TILES):
+            if nt + 1 < N_TILES:
+                prepare_adjacency(nt + 1)
+            for g in range(Q):
+                multiply(nt, g)

@@ -14,9 +14,11 @@ P = 128
 PACK = 4
 GROUP = C // Q
 N_TILES = N // P
+T_PAIRS = T // 2
 T_BANK = 4
 T_HALVES = T // T_BANK
 BANK = 512
+PSUM_BANKS = 8
 
 SIGN = (
     (+1, -1, -1, -1),
@@ -41,8 +43,9 @@ def tile_nconv_pa_t_kernel(tc, x, Ar, Ai, Aj, Ak, out):
     with ExitStack() as stack:
         keep = stack.enter_context(tc.tile_pool(name="keep", bufs=1))
         a_stage = stack.enter_context(tc.tile_pool(name="a_stage", bufs=2))
-        o_stage = stack.enter_context(tc.tile_pool(name="o_stage", bufs=4))
-        psum = stack.enter_context(tc.psum_pool(name="psum", bufs=4))
+        o_stage = stack.enter_context(tc.tile_pool(name="o_stage", bufs=2))
+        psum = stack.enter_context(tc.psum_pool(name="psum", bufs=PSUM_BANKS))
+        stack.enter_context(tc.manual_schedule())
 
         ident = keep.tile([P, P], F32)
         make_identity(nc, ident[:])
@@ -68,52 +71,51 @@ def tile_nconv_pa_t_kernel(tc, x, Ar, Ai, Aj, Ak, out):
         for nt in range(1, N_TILES):
             a_raw.append(load_adjacency(nt))
 
+        pair_width = 2 * P * PACK
         x_grouped = [
-            keep.tile([P, T * P * PACK], BF16, name="x_grouped_%d" % g, align_bytes=64)
+            keep.tile([P, T_PAIRS * pair_width], BF16, name="x_grouped_%d" % g, align_bytes=64)
             for g in range(Q)
         ]
         x_codes = [
             [
-                keep.tile([P, T_BANK * P], U32, name="x_codes_%d_%d" % (g, h), align_bytes=64)
-                for h in range(T_HALVES)
+                keep.tile([P, 2 * P], U32, name="x_codes_%d_%d" % (g, w), align_bytes=64)
+                for w in range(T_PAIRS)
             ]
             for g in range(Q)
         ]
         x_scales = [
             [
-                keep.tile([P, T_BANK * P], U8, name="x_scales_%d_%d" % (g, h), align_bytes=64)
-                for h in range(T_HALVES)
+                keep.tile([P, 2 * P], U8, name="x_scales_%d_%d" % (g, w), align_bytes=64)
+                for w in range(T_PAIRS)
             ]
             for g in range(Q)
         ]
 
-        def regroup_x(g, h):
+        def transpose_x(g, w):
             words = x_raw[g][:].bitcast(F32).rearrange(
-                "p (u q e w) -> p u q e w", u=2, q=P, e=2, w=T // 2
+                "p (u q e w) -> p u q e w", u=2, q=P, e=2, w=T_PAIRS
             )
-            grouped = x_grouped[g][:].rearrange("p (t c j) -> p t c j", t=T, c=P, j=PACK)
-            for w in range(2 * h, 2 * h + 2):
-                bank = psum.tile([P, BANK], F32, tag="transposed")
-                for u in range(2):
-                    for e in range(2):
-                        j = 2 * u + e
-                        nc.tensor.transpose(
-                            bank[:, j * P : (j + 1) * P], words[:, u, :, e, w], ident[:]
-                        )
-                halves = bank[:].bitcast(BF16).rearrange(
-                    "p (j c s) -> p s c j", j=PACK, c=P, s=2
-                )
-                if w % 2 == 0:
-                    nc.scalar.copy(out=grouped[:, 2 * w : 2 * w + 2, :, :], in_=halves)
-                else:
-                    nc.vector.tensor_copy(out=grouped[:, 2 * w : 2 * w + 2, :, :], in_=halves)
+            bank = psum.tile([P, BANK], F32, tag="bank")
+            for u in range(2):
+                for e in range(2):
+                    j = 2 * u + e
+                    nc.tensor.transpose(
+                        bank[:, j * P : (j + 1) * P], words[:, u, :, e, w], ident[:]
+                    )
+            return bank
 
-        def quantise_x(g, h):
-            width = T_BANK * P * PACK
+        def regroup_x(copy, g, w, bank):
+            target = x_grouped[g][:, w * pair_width : (w + 1) * pair_width]
+            copy(
+                out=target.rearrange("p (s c j) -> p s c j", s=2, c=P, j=PACK),
+                in_=bank[:].bitcast(BF16).rearrange("p (j c s) -> p s c j", j=PACK, c=P, s=2),
+            )
+
+        def quantise_x(g, w):
             nc.vector.quantize_mx(
-                out=x_codes[g][h][:].bitcast(FP8X4),
-                scales=x_scales[g][h][:],
-                in_=x_grouped[g][:, h * width : (h + 1) * width],
+                out=x_codes[g][w][:].bitcast(FP8X4),
+                scales=x_scales[g][w][:],
+                in_=x_grouped[g][:, w * pair_width : (w + 1) * pair_width],
             )
 
         a_codes = [
@@ -131,7 +133,7 @@ def tile_nconv_pa_t_kernel(tc, x, Ar, Ai, Aj, Ak, out):
                 "p (s n u) -> p s n u", s=SLOTS, n=P, u=2
             )
             for pair in range(2):
-                bank = psum.tile([P, BANK], F32, tag="transposed")
+                bank = psum.tile([P, BANK], F32, tag="bank")
                 for i in range(2):
                     words = a_raw[nt][2 * pair + i][:].bitcast(F32)
                     for u in range(2):
@@ -156,29 +158,31 @@ def tile_nconv_pa_t_kernel(tc, x, Ar, Ai, Aj, Ak, out):
                     in_=grouped[:, first * slot_width : (first + count) * slot_width],
                 )
 
-        def multiply(nt, g):
-            result = o_stage.tile([P, P * T], F32)
-            result_nt = result[:].rearrange("p (n t) -> p n t", n=P, t=T)
-            for h in range(T_HALVES):
-                acc = psum.tile([P, BANK], F32, tag="acc")
-                for tl in range(T_BANK):
-                    for a in range(Q):
-                        s = slot_of(g, a)
-                        nc.tensor.matmul_mx(
-                            out=acc[:, tl * P : (tl + 1) * P],
-                            lhsT=x_codes[g ^ a][h][:, tl * P : (tl + 1) * P].bitcast(FP8X4),
-                            lhsT_scale=x_scales[g ^ a][h][:, tl * P : (tl + 1) * P],
-                            rhs=a_codes[nt][:, s * P : (s + 1) * P].bitcast(FP8X4),
-                            rhs_scale=a_scales[nt][:, s * P : (s + 1) * P],
-                            start=(a == 0),
-                            stop=(a == Q - 1),
-                        )
-                by_node = acc[:].rearrange("p (t n) -> p n t", t=T_BANK, n=P)
-                target = result_nt[:, :, h * T_BANK : (h + 1) * T_BANK]
-                if (nt * Q + g) % 2 == 0:
-                    nc.scalar.copy(out=target, in_=by_node)
-                else:
-                    nc.vector.tensor_copy(out=target, in_=by_node)
+        def multiply(nt, g, h, result):
+            acc = psum.tile([P, BANK], F32, tag="bank")
+            for tl in range(T_BANK):
+                t = h * T_BANK + tl
+                w, s = t // 2, t % 2
+                for a in range(Q):
+                    k = slot_of(g, a)
+                    nc.tensor.matmul_mx(
+                        out=acc[:, tl * P : (tl + 1) * P],
+                        lhsT=x_codes[g ^ a][w][:, s * P : (s + 1) * P].bitcast(FP8X4),
+                        lhsT_scale=x_scales[g ^ a][w][:, s * P : (s + 1) * P],
+                        rhs=a_codes[nt][:, k * P : (k + 1) * P].bitcast(FP8X4),
+                        rhs_scale=a_scales[nt][:, k * P : (k + 1) * P],
+                        start=(a == 0),
+                        stop=(a == Q - 1),
+                    )
+            copy = nc.scalar.copy if g % 2 == 0 else nc.vector.tensor_copy
+            copy(
+                out=result[:].rearrange("p (n t) -> p n t", n=P, t=T)[
+                    :, :, h * T_BANK : (h + 1) * T_BANK
+                ],
+                in_=acc[:].rearrange("p (t n) -> p n t", t=T_BANK, n=P),
+            )
+
+        def store(nt, g, result):
             for b in range(B):
                 nc.sync.dma_start(
                     out=out[
@@ -188,14 +192,30 @@ def tile_nconv_pa_t_kernel(tc, x, Ar, Ai, Aj, Ak, out):
                 )
 
         prepare_adjacency(0)
-        units = [(g, h) for g in range(Q) for h in range(T_HALVES)]
-        for k, (g, h) in enumerate(units):
-            regroup_x(g, h)
-            if k > 0:
-                quantise_x(*units[k - 1])
-        quantise_x(*units[-1])
+        parked = []
+        for g in range(Q):
+            banks = [transpose_x(g, w) for w in range(T_PAIRS)]
+            regroup_x(nc.scalar.copy, g, 0, banks[0])
+            regroup_x(nc.vector.tensor_copy, g, 1, banks[1])
+            quantise_x(g, 0)
+            quantise_x(g, 1)
+            regroup_x(nc.scalar.copy, g, 2, banks[2])
+            if g > 0:
+                quantise_x(g - 1, 2)
+            parked.append(banks[3])
+        quantise_x(Q - 1, 2)
+        for g in range(Q):
+            regroup_x(nc.scalar.copy, g, 3, parked[g])
+            quantise_x(g, 3)
+
         for nt in range(N_TILES):
-            if nt + 1 < N_TILES:
-                prepare_adjacency(nt + 1)
-            for g in range(Q):
-                multiply(nt, g)
+            results = [
+                o_stage.tile([P, P * T], F32, name="result_%d" % g) for g in range(Q)
+            ]
+            for h in range(T_HALVES):
+                for g in range(Q):
+                    multiply(nt, g, h, results[g])
+                    if h == T_HALVES - 1:
+                        store(nt, g, results[g])
+                if h == 0 and nt + 1 < N_TILES:
+                    prepare_adjacency(nt + 1)

@@ -212,10 +212,13 @@ def tile_nconv_pa_t_kernel(tc, x, Ar, Ai, Aj, Ak, out):
             results = [
                 o_stage.tile([P, P * T], F32, name="result_%d" % g) for g in range(Q)
             ]
-            for h in range(T_HALVES):
-                for g in range(Q):
-                    multiply(nt, g, h, results[g])
-                    if h == T_HALVES - 1:
-                        store(nt, g, results[g])
-                if h == 0 and nt + 1 < N_TILES:
+            if nt == 0:
+                order = [(g, h) for h in range(T_HALVES) for g in range(Q)]
+            else:
+                order = [(g, h) for g in range(Q) for h in range(T_HALVES)]
+            for i, (g, h) in enumerate(order):
+                multiply(nt, g, h, results[g])
+                if h == T_HALVES - 1:
+                    store(nt, g, results[g])
+                if i + 1 == len(order) // 2 and nt + 1 < N_TILES:
                     prepare_adjacency(nt + 1)

@@ -19,6 +19,7 @@ T_BANK = 4
 T_HALVES = T // T_BANK
 BANK = 512
 PSUM_BANKS = 8
+SQUARE = 32
 
 SIGN = (
     (+1, -1, -1, -1),
@@ -50,15 +51,11 @@ def tile_nconv_pa_t_kernel(tc, x, Ar, Ai, Aj, Ak, out):
         ident = keep.tile([P, P], F32)
         make_identity(nc, ident[:])
 
-        def load_adjacency(nt):
-            tiles = []
-            for a in range(Q):
-                raw = keep.tile([P, N], BF16, name="a_raw_%d_%d" % (nt, a))
-                nc.sync.dma_start(out=raw[:], in_=adjacency[a][nt * P : (nt + 1) * P, :])
-                tiles.append(raw)
-            return tiles
-
-        a_raw = [load_adjacency(0)]
+        a_rows = []
+        for a in range(Q):
+            rows = keep.tile([P, N], BF16, name="a_rows_%d" % a)
+            nc.sync.dma_start(out=rows[:], in_=adjacency[a][0:P, :])
+            a_rows.append(rows)
         x_raw = []
         for g in range(Q):
             raw = keep.tile([P, N * T], BF16, name="x_raw_%d" % g)
@@ -68,8 +65,23 @@ def tile_nconv_pa_t_kernel(tc, x, Ar, Ai, Aj, Ak, out):
                     in_=x[b, g * GROUP : (g + 1) * GROUP].rearrange("c m t -> c (m t)"),
                 )
             x_raw.append(raw)
+        a_blocks = {}
         for nt in range(1, N_TILES):
-            a_raw.append(load_adjacency(nt))
+            blocks = keep.tile([P, Q * N], BF16, name="a_blocks_%d" % nt, align_bytes=64)
+            for a in range(Q):
+                half_rows = adjacency[a][nt * P : (nt + 1) * P, :].rearrange(
+                    "n (u i) -> (n u) i", u=2
+                )
+                for d in range(P // SQUARE):
+                    nc.sync.dma_start(
+                        out=blocks[
+                            d * SQUARE : (d + 1) * SQUARE, a * N : (a + 1) * N
+                        ].rearrange("k (f i) -> k f i", i=2 * SQUARE),
+                        in_=half_rows[:, d * 2 * SQUARE : (d + 1) * 2 * SQUARE].rearrange(
+                            "(f k) i -> k f i", k=SQUARE
+                        ),
+                    )
+            a_blocks[nt] = blocks
 
         pair_width = 2 * P * PACK
         x_grouped = [
@@ -127,15 +139,17 @@ def tile_nconv_pa_t_kernel(tc, x, Ar, Ai, Aj, Ak, out):
             for nt in range(N_TILES)
         ]
 
-        def prepare_adjacency(nt):
-            grouped = a_stage.tile([P, SLOTS * P * PACK], BF16, align_bytes=64)
+        slot_width = P * PACK
+
+        def transpose_on_tensor():
+            grouped = a_stage.tile([P, SLOTS * slot_width], BF16, tag="grouped", align_bytes=64)
             grouped_words = grouped[:].bitcast(F32).rearrange(
                 "p (s n u) -> p s n u", s=SLOTS, n=P, u=2
             )
             for pair in range(2):
                 bank = psum.tile([P, BANK], F32, tag="bank")
                 for i in range(2):
-                    words = a_raw[nt][2 * pair + i][:].bitcast(F32)
+                    words = a_rows[2 * pair + i][:].bitcast(F32)
                     for u in range(2):
                         k = 2 * i + u
                         nc.tensor.transpose(
@@ -145,7 +159,17 @@ def tile_nconv_pa_t_kernel(tc, x, Ar, Ai, Aj, Ak, out):
                     out=grouped_words[:, 2 * pair : 2 * pair + 2, :, :],
                     in_=bank[:].rearrange("p (s u n) -> p s n u", s=2, u=2, n=P),
                 )
-            slot_width = P * PACK
+            return grouped
+
+        def transpose_on_vector(nt):
+            grouped = a_stage.tile([P, SLOTS * slot_width], BF16, tag="grouped", align_bytes=64)
+            nc.vector.transpose(
+                out=grouped[:].bitcast(F32)[:, 0 : Q * slot_width // 2],
+                in_=a_blocks[nt][:].bitcast(F32),
+            )
+            return grouped
+
+        def quantise_adjacency(nt, grouped):
             nc.vector.tensor_scalar_mul(
                 out=grouped[:, Q * slot_width : SLOTS * slot_width],
                 in0=grouped[:, slot_width : Q * slot_width],
@@ -191,7 +215,7 @@ def tile_nconv_pa_t_kernel(tc, x, Ar, Ai, Aj, Ak, out):
                     in_=result[b:P:B, :],
                 )
 
-        prepare_adjacency(0)
+        quantise_adjacency(0, transpose_on_tensor())
         parked = []
         for g in range(Q):
             banks = [transpose_x(g, w) for w in range(T_PAIRS)]
@@ -212,13 +236,10 @@ def tile_nconv_pa_t_kernel(tc, x, Ar, Ai, Aj, Ak, out):
             results = [
                 o_stage.tile([P, P * T], F32, name="result_%d" % g) for g in range(Q)
             ]
-            if nt == 0:
-                order = [(g, h) for h in range(T_HALVES) for g in range(Q)]
-            else:
-                order = [(g, h) for g in range(Q) for h in range(T_HALVES)]
-            for i, (g, h) in enumerate(order):
-                multiply(nt, g, h, results[g])
-                if h == T_HALVES - 1:
-                    store(nt, g, results[g])
-                if i + 1 == len(order) // 2 and nt + 1 < N_TILES:
-                    prepare_adjacency(nt + 1)
+            for h in range(T_HALVES):
+                for g in range(Q):
+                    multiply(nt, g, h, results[g])
+                    if h == T_HALVES - 1:
+                        store(nt, g, results[g])
+                if h == 0 and nt + 1 < N_TILES:
+                    quantise_adjacency(nt + 1, transpose_on_vector(nt + 1))

from contextlib import ExitStack

import concourse.mybir as mybir
from concourse.masks import make_identity

F32 = mybir.dt.float32
BF16 = mybir.dt.bfloat16
U32 = mybir.dt.uint32
U8 = mybir.dt.uint8
FP8X4 = mybir.dt.float8_e4m3fn_x4

B, C, N, T, Q = 4, 128, 512, 8, 4
P = 128
PACK = 4
GROUP = C // Q
N_TILES = N // P
T_PAIRS = T // 2
T_BANK = 4
T_HALVES = T // T_BANK
BANK = 512
PSUM_BANKS = 8
SQUARE = 32

SIGN = (
    (+1, -1, -1, -1),
    (+1, +1, +1, -1),
    (+1, -1, +1, +1),
    (+1, +1, -1, +1),
)
SLOTS = 2 * Q - 1
SLOT_RUNS = ((0, 4), (4, 2), (6, 1))

FLOPS = 2 * Q * N * N * B * C * T


def slot_of(g, a):
    return a if SIGN[g][a] > 0 else Q - 1 + a


def tile_nconv_pa_t_kernel(tc, x, Ar, Ai, Aj, Ak, out):
    nc = tc.nc
    adjacency = (Ar, Ai, Aj, Ak)

    with ExitStack() as stack:
        keep = stack.enter_context(tc.tile_pool(name="keep", bufs=1))
        a_stage = stack.enter_context(tc.tile_pool(name="a_stage", bufs=2))
        o_stage = stack.enter_context(tc.tile_pool(name="o_stage", bufs=2))
        psum = stack.enter_context(tc.psum_pool(name="psum", bufs=PSUM_BANKS))
        stack.enter_context(tc.manual_schedule())

        ident = keep.tile([P, P], F32)
        make_identity(nc, ident[:])

        a_rows = []
        for a in range(Q):
            rows = keep.tile([P, N], BF16, name="a_rows_%d" % a)
            nc.sync.dma_start(out=rows[:], in_=adjacency[a][0:P, :])
            a_rows.append(rows)
        x_raw = []
        for g in range(Q):
            raw = keep.tile([P, N * T], BF16, name="x_raw_%d" % g)
            for b in range(B):
                nc.sync.dma_start(
                    out=raw[b:P:B, :],
                    in_=x[b, g * GROUP : (g + 1) * GROUP].rearrange("c m t -> c (m t)"),
                )
            x_raw.append(raw)
        a_blocks = {}
        for nt in range(1, N_TILES):
            blocks = keep.tile([P, Q * N], BF16, name="a_blocks_%d" % nt, align_bytes=64)
            for a in range(Q):
                half_rows = adjacency[a][nt * P : (nt + 1) * P, :].rearrange(
                    "n (u i) -> (n u) i", u=2
                )
                for d in range(P // SQUARE):
                    nc.sync.dma_start(
                        out=blocks[
                            d * SQUARE : (d + 1) * SQUARE, a * N : (a + 1) * N
                        ].rearrange("k (f i) -> k f i", i=2 * SQUARE),
                        in_=half_rows[:, d * 2 * SQUARE : (d + 1) * 2 * SQUARE].rearrange(
                            "(f k) i -> k f i", k=SQUARE
                        ),
                    )
            a_blocks[nt] = blocks

        pair_width = 2 * P * PACK
        x_grouped = [
            keep.tile([P, T_PAIRS * pair_width], BF16, name="x_grouped_%d" % g, align_bytes=64)
            for g in range(Q)
        ]
        x_codes = [
            [
                keep.tile([P, 2 * P], U32, name="x_codes_%d_%d" % (g, w), align_bytes=64)
                for w in range(T_PAIRS)
            ]
            for g in range(Q)
        ]
        x_scales = [
            [
                keep.tile([P, 2 * P], U8, name="x_scales_%d_%d" % (g, w), align_bytes=64)
                for w in range(T_PAIRS)
            ]
            for g in range(Q)
        ]

        def transpose_x(g, w):
            words = x_raw[g][:].bitcast(F32).rearrange(
                "p (u q e w) -> p u q e w", u=2, q=P, e=2, w=T_PAIRS
            )
            bank = psum.tile([P, BANK], F32, tag="bank")
            for u in range(2):
                for e in range(2):
                    j = 2 * u + e
                    nc.tensor.transpose(
                        bank[:, j * P : (j + 1) * P], words[:, u, :, e, w], ident[:]
                    )
            return bank

        def regroup_x(copy, g, w, bank):
            target = x_grouped[g][:, w * pair_width : (w + 1) * pair_width]
            copy(
                out=target.rearrange("p (s c j) -> p s c j", s=2, c=P, j=PACK),
                in_=bank[:].bitcast(BF16).rearrange("p (j c s) -> p s c j", j=PACK, c=P, s=2),
            )

        def quantise_x(g, w):
            nc.vector.quantize_mx(
                out=x_codes[g][w][:].bitcast(FP8X4),
                scales=x_scales[g][w][:],
                in_=x_grouped[g][:, w * pair_width : (w + 1) * pair_width],
            )

        a_codes = [
            keep.tile([P, SLOTS * P], U32, name="a_codes_%d" % nt, align_bytes=64)
            for nt in range(N_TILES)
        ]
        a_scales = [
            keep.tile([P, SLOTS * P], U8, name="a_scales_%d" % nt, align_bytes=64)
            for nt in range(N_TILES)
        ]

        slot_width = P * PACK

        def transpose_on_tensor():
            grouped = a_stage.tile([P, SLOTS * slot_width], BF16, tag="grouped", align_bytes=64)
            grouped_words = grouped[:].bitcast(F32).rearrange(
                "p (s n u) -> p s n u", s=SLOTS, n=P, u=2
            )
            for pair in range(2):
                bank = psum.tile([P, BANK], F32, tag="bank")
                for i in range(2):
                    words = a_rows[2 * pair + i][:].bitcast(F32)
                    for u in range(2):
                        k = 2 * i + u
                        nc.tensor.transpose(
                            bank[:, k * P : (k + 1) * P], words[:, u * P : (u + 1) * P], ident[:]
                        )
                nc.scalar.copy(
                    out=grouped_words[:, 2 * pair : 2 * pair + 2, :, :],
                    in_=bank[:].rearrange("p (s u n) -> p s n u", s=2, u=2, n=P),
                )
            return grouped

        def transpose_on_vector(nt):
            grouped = a_stage.tile([P, SLOTS * slot_width], BF16, tag="grouped", align_bytes=64)
            nc.vector.transpose(
                out=grouped[:].bitcast(F32)[:, 0 : Q * slot_width // 2],
                in_=a_blocks[nt][:].bitcast(F32),
            )
            return grouped

        def quantise_adjacency(nt, grouped):
            nc.vector.tensor_scalar_mul(
                out=grouped[:, Q * slot_width : SLOTS * slot_width],
                in0=grouped[:, slot_width : Q * slot_width],
                scalar1=-1.0,
            )
            for first, count in SLOT_RUNS:
                nc.vector.quantize_mx(
                    out=a_codes[nt][:, first * P : (first + count) * P].bitcast(FP8X4),
                    scales=a_scales[nt][:, first * P : (first + count) * P],
                    in_=grouped[:, first * slot_width : (first + count) * slot_width],
                )

        def multiply(nt, g, h, result):
            acc = psum.tile([P, BANK], F32, tag="bank")
            for tl in range(T_BANK):
                t = h * T_BANK + tl
                w, s = t // 2, t % 2
                for a in range(Q):
                    k = slot_of(g, a)
                    nc.tensor.matmul_mx(
                        out=acc[:, tl * P : (tl + 1) * P],
                        lhsT=x_codes[g ^ a][w][:, s * P : (s + 1) * P].bitcast(FP8X4),
                        lhsT_scale=x_scales[g ^ a][w][:, s * P : (s + 1) * P],
                        rhs=a_codes[nt][:, k * P : (k + 1) * P].bitcast(FP8X4),
                        rhs_scale=a_scales[nt][:, k * P : (k + 1) * P],
                        start=(a == 0),
                        stop=(a == Q - 1),
                    )
            copy = nc.scalar.copy if g % 2 == 0 else nc.vector.tensor_copy
            copy(
                out=result[:].rearrange("p (n t) -> p n t", n=P, t=T)[
                    :, :, h * T_BANK : (h + 1) * T_BANK
                ],
                in_=acc[:].rearrange("p (t n) -> p n t", t=T_BANK, n=P),
            )

        def store(nt, g, result):
            for b in range(B):
                nc.sync.dma_start(
                    out=out[
                        b, g * GROUP : (g + 1) * GROUP, nt * P : (nt + 1) * P, :
                    ].rearrange("c n t -> c (n t)"),
                    in_=result[b:P:B, :],
                )

        quantise_adjacency(0, transpose_on_tensor())
        parked = []
        for g in range(Q):
            banks = [transpose_x(g, w) for w in range(T_PAIRS)]
            regroup_x(nc.scalar.copy, g, 0, banks[0])
            regroup_x(nc.vector.tensor_copy, g, 1, banks[1])
            quantise_x(g, 0)
            quantise_x(g, 1)
            regroup_x(nc.scalar.copy, g, 2, banks[2])
            if g > 0:
                quantise_x(g - 1, 2)
            parked.append(banks[3])
        quantise_x(Q - 1, 2)
        for g in range(Q):
            regroup_x(nc.scalar.copy, g, 3, parked[g])
            quantise_x(g, 3)

        for nt in range(N_TILES):
            results = [
                o_stage.tile([P, P * T], F32, name="result_%d" % g) for g in range(Q)
            ]
            for h in range(T_HALVES):
                for g in range(Q):
                    multiply(nt, g, h, results[g])
                    if h == T_HALVES - 1:
                        store(nt, g, results[g])
                if h == 0 and nt + 1 < N_TILES:
                    quantise_adjacency(nt + 1, transpose_on_vector(nt + 1))
